import numpy as np
import ml_dtypes


def mxq(x, axis, fmt="e4m3"):
    dtype, down = {"e4m3": (ml_dtypes.float8_e4m3fn, 7), "e5m2": (ml_dtypes.float8_e5m2, 14)}[fmt]
    v = np.moveaxis(np.asarray(x, np.float32).astype(ml_dtypes.bfloat16).astype(np.float64), axis, -1)
    blocks = v.reshape(v.shape[:-1] + (-1, 32))
    amax = np.abs(blocks).max(-1, keepdims=True)
    byte = np.maximum(np.where(amax > 0, np.frexp(amax)[1] - 1 + 127, 0) - down, 1)
    scale = np.exp2(byte - 127.0)
    codes = (blocks / scale).astype(np.float32).astype(dtype).astype(np.float64)
    return np.moveaxis((codes * scale).reshape(v.shape), -1, axis)


WIDE = False


def mx_kscale(k):
    if not WIDE:
        return np.ones(k)
    levels = np.array([10, -10, 5, -5, 0])
    a = np.random.permutation(np.resize(levels, k // 512 * 4)).reshape(k // 512, 4)
    idx = np.arange(k)
    return np.exp2(a[idx // 512, idx % 128 // 32])


BF16 = ml_dtypes.bfloat16


def bf(x):
    return np.asarray(x, np.float32).astype(BF16)


def f64(x):
    return np.asarray(x).astype(np.float64)


E2M1 = np.array([0.0, 0.5, 1.0, 1.5, 2.0, 3.0, 4.0, 6.0, -0.0, -0.5, -1.0, -1.5, -2.0, -3.0, -4.0, -6.0])


def pack_weight(w, fmt):
    k, n = w.shape
    w = f64(bf(w)).reshape(k // 32, 32, n)
    amax = np.abs(w).max(1)
    if fmt == "e4m3":
        byte = np.frexp(amax)[1] - 1 + 127 - 7
    else:
        mant, ex = np.frexp(amax / 6.0)
        byte = np.where(mant > 0.5, ex, ex - 1) + 127
    byte = np.clip(np.where(amax > 0, byte, 1), 1, 254)
    scaled = (w * np.exp2(127.0 - byte)[:, None, :]).reshape(k, n).astype(np.float32)
    by_word = np.ascontiguousarray(scaled.reshape(k // 512, 128, 4, n).transpose(0, 1, 3, 2))
    if fmt == "e4m3":
        words = by_word.astype(ml_dtypes.float8_e4m3fn).view(np.uint8)
    else:
        c = by_word.astype(ml_dtypes.float4_e2m1fn).view(np.uint8) & 0xF
        words = c[..., 0::2] | (c[..., 1::2] << 4)
    return np.ascontiguousarray(words), np.ascontiguousarray(byte.astype(np.uint8).reshape(k // 512, 16, n))


def unpack_weight(words, scales, fmt):
    g, p, n, _ = words.shape
    if fmt == "e4m3":
        vals = np.ascontiguousarray(words).view(ml_dtypes.float8_e4m3fn).astype(np.float64)
    else:
        nib = np.empty((g, p, n, 4), np.uint8)
        nib[..., 0::2] = words & 0xF
        nib[..., 1::2] = words >> 4
        vals = E2M1[nib]
    vals = vals * np.repeat(np.exp2(scales.astype(np.float64) - 127.0), 8, axis=1)[..., None]
    return vals.transpose(0, 1, 3, 2).reshape(g * 512, n)

def pack4(w):
    words, scales = pack_weight(w, "e2m1")
    return words.reshape(words.shape[0], 128, -1), scales


def unpack4(words, scales):
    return unpack_weight(words.reshape(words.shape[0], 128, -1, 2), scales, "e2m1")


B, T, C, H, G = 2, 128, 512, 16, 16
HS = C // H
TG = T // G
THETA = 10000.0


def apply_rope(t, cos, sin):
    tp = t.reshape(B, T, H, HS // 2, 2)
    a, b = tp[..., 0], tp[..., 1]
    c = cos[None, :, None, :]
    s = sin[None, :, None, :]
    return np.stack([a * c - b * s, a * s + b * c], axis=-1).reshape(B, T, H, HS)


def grp(t):
    return t.reshape(B, G, TG, H, HS).transpose(0, 3, 1, 2, 4)


def with_summary(t):
    return np.concatenate([t, t.mean(axis=3, keepdims=True)], axis=3)


def setup_inputs():
    s = mx_kscale(C)
    x = np.random.standard_normal((B, T, C)) * 0.7 + np.random.standard_normal((B, 1, C)) * 0.7
    w = np.random.standard_normal((3 * C, C)) / np.sqrt(C)
    ang = np.arange(T)[:, None] / THETA ** (np.arange(0, HS, 2) / HS)[None, :]
    words, scales = pack4((w / s[None, :]).T)
    return {"x": bf(x * s), "w_attn_words": words, "w_attn_scales": scales, "freqs_cos": bf(np.cos(ang)), "freqs_sin": bf(np.sin(ang))}


def reference(x, w_attn_words, w_attn_scales, freqs_cos, freqs_sin):
    cos, sin = f64(freqs_cos), f64(freqs_sin)
    qkv = mxq(f64(x), 2, "e4m3") @ unpack4(w_attn_words, w_attn_scales)
    q, k, v = np.split(qkv, 3, axis=2)
    q = apply_rope(q.reshape(B, T, H, HS), cos, sin).reshape(B, T, C)
    k = apply_rope(k.reshape(B, T, H, HS), cos, sin).reshape(B, T, C)
    q, k, v = grp(q), grp(k), grp(v)
    return with_summary(q), with_summary(k), with_summary(v)

@@ -1,0 +1,210 @@
+from contextlib import ExitStack
+
+import concourse.mybir as mybir
+from concourse.masks import make_identity
+
+F32 = mybir.dt.float32
+BF16 = mybir.dt.bfloat16
+I32 = mybir.dt.int32
+U8 = mybir.dt.uint8
+U32 = mybir.dt.uint32
+FP8X4 = mybir.dt.float8_e4m3fn_x4
+FP4X4 = mybir.dt.float4_e2m1fn_x4
+MULT = mybir.AluOpType.mult
+
+P = 128
+BATCH = 2
+POSITIONS = 128
+CHANNELS = 512
+GROUPS = 16
+GROUP = 8
+HEAD = 32
+PAIRS = HEAD // 2
+BLOCK_HEADS = P // HEAD
+HEAD_BLOCKS = CHANNELS // P
+TENSORS = 3
+ROTATED = 2
+HALVES = 2
+HALF = GROUP // HALVES
+TOKENS = BATCH * POSITIONS
+HALF_TOKENS = TOKENS // HALVES
+
+FLOPS = 2 * TOKENS * CHANNELS * TENSORS * CHANNELS
+
+
+def tile_causalselfattention2_pa_s_kernel(
+    tc, x, w_attn_words, w_attn_scales, freqs_cos, freqs_sin, out_0, out_1, out_2
+):
+    nc = tc.nc
+    outs = (out_0, out_1, out_2)
+    with ExitStack() as ctx:
+        keep = ctx.enter_context(tc.tile_pool(name="keep", bufs=1))
+        work = ctx.enter_context(tc.tile_pool(name="work", bufs=ROTATED * HALVES))
+        banks = ctx.enter_context(tc.psum_pool(name="banks", bufs=8))
+
+        x_rows = keep.tile([P, BATCH, CHANNELS], BF16)
+        nc.sync.dma_start(out=x_rows[:], in_=x.rearrange("b t c -> t b c"))
+        cos_rows = keep.tile([P, PAIRS], BF16)
+        sin_rows = keep.tile([P, PAIRS], BF16)
+        nc.scalar.dma_start(out=cos_rows[:], in_=freqs_cos)
+        nc.scalar.dma_start(out=sin_rows[:], in_=freqs_sin)
+
+        w_scales = keep.tile([P, TENSORS * CHANNELS], U8, align_bytes=64)
+        nc.vector.memset(w_scales[:].bitcast(I32), 0)
+        for quadrant in range(4):
+            nc.sync.dma_start(
+                out=w_scales[32 * quadrant : 32 * quadrant + 4, :].bitcast(I32),
+                in_=w_attn_scales[0, 4 * quadrant : 4 * quadrant + 4, :].bitcast(I32),
+            )
+        w_words = keep.tile([P, 2 * TENSORS * CHANNELS], U8, align_bytes=64)
+        for s in range(TENSORS):
+            tensor_bytes = slice(2 * CHANNELS * s, 2 * CHANNELS * (s + 1))
+            nc.sync.dma_start(
+                out=w_words[:, tensor_bytes].bitcast(I32),
+                in_=w_attn_words[0, :, tensor_bytes].bitcast(I32),
+            )
+
+        identity = keep.tile([P, P], F32)
+        make_identity(nc, identity[:])
+        swap_pairs = keep.tile([P, P], F32)
+        identity_pairs = identity[:].rearrange("p (m e) -> p m e", e=2)
+        swapped_pairs = swap_pairs[:].rearrange("p (m e) -> p m e", e=2)
+        nc.gpsimd.tensor_copy(out=swapped_pairs[:, :, 0], in_=identity_pairs[:, :, 1])
+        nc.gpsimd.tensor_copy(out=swapped_pairs[:, :, 1], in_=identity_pairs[:, :, 0])
+
+        cos_wide = keep.tile([P, BLOCK_HEADS, PAIRS, 2], F32)
+        sin_wide = keep.tile([P, BLOCK_HEADS, PAIRS, 2], F32)
+        nc.vector.tensor_copy(
+            out=cos_wide[:],
+            in_=cos_rows[:].unsqueeze(1).unsqueeze(3).to_broadcast([P, BLOCK_HEADS, PAIRS, 2]),
+        )
+        sin_heads = sin_rows[:].unsqueeze(1).to_broadcast([P, BLOCK_HEADS, PAIRS])
+        nc.vector.tensor_copy(out=sin_wide[:, :, :, 0], in_=sin_heads)
+        nc.vector.tensor_scalar_mul(out=sin_wide[:, :, :, 1], in0=sin_heads, scalar1=-1.0)
+        factors_bank = banks.tile([P, 2, POSITIONS], F32, tag="bank")
+        nc.tensor.transpose(
+            factors_bank[:, 0, :], cos_wide[:].rearrange("p f i e -> p (f i e)"), identity[:]
+        )
+        nc.tensor.transpose(
+            factors_bank[:, 1, :], sin_wide[:].rearrange("p f i e -> p (f i e)"), identity[:]
+        )
+        factors = keep.tile([P, 2, GROUP, GROUPS, BATCH], F32)
+        for which in range(2):
+            nc.scalar.copy(
+                out=factors[:, which],
+                in_=factors_bank[:, which, :]
+                .rearrange("p (g r) -> p r g", r=GROUP)
+                .unsqueeze(3)
+                .to_broadcast([P, GROUP, GROUPS, BATCH]),
+            )
+
+        x_words = x_rows[:].bitcast(F32)
+        x_bank = banks.tile([P, BATCH, 2, POSITIONS], F32, tag="bank")
+        for b in range(BATCH):
+            for u in range(2):
+                nc.tensor.transpose(
+                    x_bank[:, b, u, :], x_words[:, b, u : CHANNELS // 2 : 2], identity[:]
+                )
+        x_grouped = keep.tile([P, TOKENS, 4], BF16, align_bytes=64)
+        x_grouped_words = (
+            x_grouped[:]
+            .rearrange("p n t -> p (n t)")
+            .bitcast(F32)
+            .rearrange("p (r g b u) -> p r g b u", r=GROUP, g=GROUPS, b=BATCH)
+        )
+        x_bank_sorted = x_bank[:].rearrange("p b u (g r) -> p r g b u", r=GROUP)
+        x_codes = keep.tile([P, TOKENS], U32, align_bytes=64)
+        x_scales = keep.tile([P, TOKENS], U8, align_bytes=64)
+        for half in range(HALVES):
+            places = slice(HALF * half, HALF * (half + 1))
+            nc.vector.tensor_copy(out=x_grouped_words[:, places], in_=x_bank_sorted[:, places])
+        for half in range(HALVES):
+            tokens = slice(HALF_TOKENS * half, HALF_TOKENS * (half + 1))
+            nc.vector.quantize_mx(
+                out=x_codes[:, tokens].bitcast(FP8X4),
+                scales=x_scales[:, tokens],
+                in_=x_grouped[:, tokens, :].rearrange("p n t -> p (n t)"),
+            )
+
+        products = {}
+        for s in range(TENSORS):
+            for half in range(HALVES):
+                tokens = slice(HALF_TOKENS * half, HALF_TOKENS * (half + 1))
+                product = banks.tile([P, HEAD_BLOCKS, HALF_TOKENS], F32, tag="bank")
+                for j in range(HEAD_BLOCKS):
+                    first = CHANNELS * s + P * j
+                    nc.tensor.matmul_mx(
+                        out=product[:, j, :],
+                        lhsT=w_words[:, 2 * first : 2 * (first + P)].bitcast(FP4X4),
+                        lhsT_scale=w_scales[:, first : first + P],
+                        rhs=x_codes[:, tokens].bitcast(FP8X4),
+                        rhs_scale=x_scales[:, tokens],
+                        start=True,
+                        stop=True,
+                    )
+                products[(s, half)] = product
+
+        for s in range(TENSORS):
+            result = keep.tile([P, BLOCK_HEADS, GROUP + 1, HEAD], F32, name="result%d" % s)
+            group_sum = banks.tile([P, P], F32, tag="bank")
+            for half in range(HALVES):
+                places = slice(HALF * half, HALF * (half + 1))
+                product = products[(s, half)][:].rearrange("p j (r n) -> p r n j", r=HALF)
+                if s < ROTATED:
+                    pieces = []
+                    for which, permutation in ((0, identity), (1, swap_pairs)):
+                        factor = (
+                            factors[:, which, places]
+                            .rearrange("p r g b -> p r (g b)")
+                            .unsqueeze(3)
+                            .to_broadcast([P, HALF, GROUPS * BATCH, HEAD_BLOCKS])
+                        )
+                        scaled = work.tile([P, HALF, P], F32, tag="scaled%d" % which)
+                        nc.vector.tensor_tensor(
+                            out=scaled[:].rearrange("p r (n j) -> p r n j", j=HEAD_BLOCKS),
+                            in0=product,
+                            in1=factor,
+                            op=MULT,
+                        )
+                        pieces.append((scaled, permutation))
+                else:
+                    plain = work.tile([P, HALF, P], F32, tag="plain")
+                    nc.scalar.copy(
+                        out=plain[:].rearrange("p r (n j) -> p r n j", j=HEAD_BLOCKS),
+                        in_=product,
+                    )
+                    pieces = [(plain, identity)]
+
+                turned = banks.tile([P, HALF, P], F32, tag="bank")
+                for r in range(HALF):
+                    for n, (piece, permutation) in enumerate(pieces):
+                        nc.tensor.matmul(
+                            out=turned[:, r, :],
+                            lhsT=piece[:, r, :],
+                            rhs=permutation[:],
+                            start=(n == 0),
+                            stop=(n == len(pieces) - 1),
+                            is_transpose=True,
+                        )
+                        nc.tensor.matmul(
+                            out=group_sum[:],
+                            lhsT=piece[:, r, :],
+                            rhs=permutation[:],
+                            start=(half == 0 and r == 0 and n == 0),
+                            stop=(half == HALVES - 1 and r == HALF - 1 and n == len(pieces) - 1),
+                            is_transpose=True,
+                        )
+                nc.scalar.copy(
+                    out=result[:, :, places, :].rearrange("p f r c -> p r f c"),
+                    in_=turned[:].rearrange("p r (f c) -> p r f c", c=HEAD),
+                )
+            nc.vector.tensor_scalar_mul(
+                out=result[:, :, GROUP, :],
+                in0=group_sum[:].rearrange("p (f c) -> p f c", c=HEAD),
+                scalar1=1.0 / GROUP,
+            )
+            groups_of = outs[s].rearrange("b (j f) g r c -> f g (b j) (r c)", f=BLOCK_HEADS)
+            for f in range(BLOCK_HEADS):
+                nc.sync.dma_start(
+                    out=groups_of[f], in_=result[:, f, :, :].rearrange("p r c -> p (r c)")
+                )

@@ -11,6 +11,8 @@ U32 = mybir.dt.uint32
 FP8X4 = mybir.dt.float8_e4m3fn_x4
 FP4X4 = mybir.dt.float4_e2m1fn_x4
 MULT = mybir.AluOpType.mult
+ADD = mybir.AluOpType.add
+AXIS_X = mybir.AxisListType.X
 
 P = 128
 BATCH = 2
@@ -42,12 +44,12 @@ def tile_causalselfattention2_pa_s_kernel(
         work = ctx.enter_context(tc.tile_pool(name="work", bufs=ROTATED * HALVES))
         banks = ctx.enter_context(tc.psum_pool(name="banks", bufs=8))
 
-        x_rows = keep.tile([P, BATCH, CHANNELS], BF16)
-        nc.sync.dma_start(out=x_rows[:], in_=x.rearrange("b t c -> t b c"))
         cos_rows = keep.tile([P, PAIRS], BF16)
         sin_rows = keep.tile([P, PAIRS], BF16)
         nc.scalar.dma_start(out=cos_rows[:], in_=freqs_cos)
         nc.scalar.dma_start(out=sin_rows[:], in_=freqs_sin)
+        x_rows = keep.tile([P, BATCH, CHANNELS], BF16)
+        nc.sync.dma_start(out=x_rows[:], in_=x.rearrange("b t c -> t b c"))
 
         w_scales = keep.tile([P, TENSORS * CHANNELS], U8, align_bytes=64)
         nc.vector.memset(w_scales[:].bitcast(I32), 0)
@@ -57,7 +59,7 @@ def tile_causalselfattention2_pa_s_kernel(
                 in_=w_attn_scales[0, 4 * quadrant : 4 * quadrant + 4, :].bitcast(I32),
             )
         w_words = keep.tile([P, 2 * TENSORS * CHANNELS], U8, align_bytes=64)
-        for s in range(TENSORS):
+        for s in (0, 2, 1):
             tensor_bytes = slice(2 * CHANNELS * s, 2 * CHANNELS * (s + 1))
             nc.sync.dma_start(
                 out=w_words[:, tensor_bytes].bitcast(I32),
@@ -81,22 +83,6 @@ def tile_causalselfattention2_pa_s_kernel(
         sin_heads = sin_rows[:].unsqueeze(1).to_broadcast([P, BLOCK_HEADS, PAIRS])
         nc.vector.tensor_copy(out=sin_wide[:, :, :, 0], in_=sin_heads)
         nc.vector.tensor_scalar_mul(out=sin_wide[:, :, :, 1], in0=sin_heads, scalar1=-1.0)
-        factors_bank = banks.tile([P, 2, POSITIONS], F32, tag="bank")
-        nc.tensor.transpose(
-            factors_bank[:, 0, :], cos_wide[:].rearrange("p f i e -> p (f i e)"), identity[:]
-        )
-        nc.tensor.transpose(
-            factors_bank[:, 1, :], sin_wide[:].rearrange("p f i e -> p (f i e)"), identity[:]
-        )
-        factors = keep.tile([P, 2, GROUP, GROUPS, BATCH], F32)
-        for which in range(2):
-            nc.scalar.copy(
-                out=factors[:, which],
-                in_=factors_bank[:, which, :]
-                .rearrange("p (g r) -> p r g", r=GROUP)
-                .unsqueeze(3)
-                .to_broadcast([P, GROUP, GROUPS, BATCH]),
-            )
 
         x_words = x_rows[:].bitcast(F32)
         x_bank = banks.tile([P, BATCH, 2, POSITIONS], F32, tag="bank")
@@ -105,6 +91,14 @@ def tile_causalselfattention2_pa_s_kernel(
                 nc.tensor.transpose(
                     x_bank[:, b, u, :], x_words[:, b, u : CHANNELS // 2 : 2], identity[:]
                 )
+        factors_bank = banks.tile([P, 2, POSITIONS], F32, tag="bank")
+        nc.tensor.transpose(
+            factors_bank[:, 0, :], cos_wide[:].rearrange("p f i e -> p (f i e)"), identity[:]
+        )
+        nc.tensor.transpose(
+            factors_bank[:, 1, :], sin_wide[:].rearrange("p f i e -> p (f i e)"), identity[:]
+        )
+
         x_grouped = keep.tile([P, TOKENS, 4], BF16, align_bytes=64)
         x_grouped_words = (
             x_grouped[:]
@@ -115,9 +109,8 @@ def tile_causalselfattention2_pa_s_kernel(
         x_bank_sorted = x_bank[:].rearrange("p b u (g r) -> p r g b u", r=GROUP)
         x_codes = keep.tile([P, TOKENS], U32, align_bytes=64)
         x_scales = keep.tile([P, TOKENS], U8, align_bytes=64)
-        for half in range(HALVES):
-            places = slice(HALF * half, HALF * (half + 1))
-            nc.vector.tensor_copy(out=x_grouped_words[:, places], in_=x_bank_sorted[:, places])
+        nc.vector.tensor_copy(out=x_grouped_words[:, 0:HALF], in_=x_bank_sorted[:, 0:HALF])
+        nc.scalar.copy(out=x_grouped_words[:, HALF:GROUP], in_=x_bank_sorted[:, HALF:GROUP])
         for half in range(HALVES):
             tokens = slice(HALF_TOKENS * half, HALF_TOKENS * (half + 1))
             nc.vector.quantize_mx(
@@ -126,66 +119,76 @@ def tile_causalselfattention2_pa_s_kernel(
                 in_=x_grouped[:, tokens, :].rearrange("p n t -> p (n t)"),
             )
 
-        products = {}
-        for s in range(TENSORS):
-            for half in range(HALVES):
-                tokens = slice(HALF_TOKENS * half, HALF_TOKENS * (half + 1))
-                product = banks.tile([P, HEAD_BLOCKS, HALF_TOKENS], F32, tag="bank")
-                for j in range(HEAD_BLOCKS):
-                    first = CHANNELS * s + P * j
-                    nc.tensor.matmul_mx(
-                        out=product[:, j, :],
-                        lhsT=w_words[:, 2 * first : 2 * (first + P)].bitcast(FP4X4),
-                        lhsT_scale=w_scales[:, first : first + P],
-                        rhs=x_codes[:, tokens].bitcast(FP8X4),
-                        rhs_scale=x_scales[:, tokens],
-                        start=True,
-                        stop=True,
-                    )
-                products[(s, half)] = product
+        factors = keep.tile([P, 2, GROUP, GROUPS, BATCH], F32)
+        for which in range(2):
+            nc.scalar.copy(
+                out=factors[:, which],
+                in_=factors_bank[:, which, :]
+                .rearrange("p (g r) -> p r g", r=GROUP)
+                .unsqueeze(3)
+                .to_broadcast([P, GROUP, GROUPS, BATCH]),
+            )
 
+        products = {}
+        for s, half in ((0, 0), (2, 0), (2, 1), (0, 1), (1, 0), (1, 1)):
+            tokens = slice(HALF_TOKENS * half, HALF_TOKENS * (half + 1))
+            product = banks.tile([P, HEAD_BLOCKS, HALF_TOKENS], F32, tag="bank")
+            for j in range(HEAD_BLOCKS):
+                first = CHANNELS * s + P * j
+                nc.tensor.matmul_mx(
+                    out=product[:, j, :],
+                    lhsT=w_words[:, 2 * first : 2 * (first + P)].bitcast(FP4X4),
+                    lhsT_scale=w_scales[:, first : first + P],
+                    rhs=x_codes[:, tokens].bitcast(FP8X4),
+                    rhs_scale=x_scales[:, tokens],
+                    start=True,
+                    stop=True,
+                )
+            products[(s, half)] = product
+
+        def sorted_product(s, half):
+            return products[(s, half)][:].rearrange("p j (r n) -> p r n j", r=HALF)
+
+        plains = []
+        for half in range(HALVES):
+            plain = work.tile([P, HALF, P], F32, tag="plain")
+            nc.scalar.copy(
+                out=plain[:].rearrange("p r (n j) -> p r n j", j=HEAD_BLOCKS),
+                in_=sorted_product(2, half),
+            )
+            plains.append(plain)
+
+        results = []
         for s in range(TENSORS):
             result = keep.tile([P, BLOCK_HEADS, GROUP + 1, HEAD], F32, name="result%d" % s)
-            group_sum = banks.tile([P, P], F32, tag="bank")
-            for half in range(HALVES):
-                places = slice(HALF * half, HALF * (half + 1))
-                product = products[(s, half)][:].rearrange("p j (r n) -> p r n j", r=HALF)
-                if s < ROTATED:
-                    pieces = []
-                    for which, permutation in ((0, identity), (1, swap_pairs)):
-                        factor = (
-                            factors[:, which, places]
-                            .rearrange("p r g b -> p r (g b)")
-                            .unsqueeze(3)
-                            .to_broadcast([P, HALF, GROUPS * BATCH, HEAD_BLOCKS])
-                        )
-                        scaled = work.tile([P, HALF, P], F32, tag="scaled%d" % which)
-                        nc.vector.tensor_tensor(
-                            out=scaled[:].rearrange("p r (n j) -> p r n j", j=HEAD_BLOCKS),
-                            in0=product,
-                            in1=factor,
-                            op=MULT,
-                        )
-                        pieces.append((scaled, permutation))
-                else:
-                    plain = work.tile([P, HALF, P], F32, tag="plain")
-                    nc.scalar.copy(
-                        out=plain[:].rearrange("p r (n j) -> p r n j", j=HEAD_BLOCKS),
-                        in_=product,
-                    )
-                    pieces = [(plain, identity)]
+            results.append(result)
 
-                turned = banks.tile([P, HALF, P], F32, tag="bank")
-                for r in range(HALF):
-                    for n, (piece, permutation) in enumerate(pieces):
-                        nc.tensor.matmul(
-                            out=turned[:, r, :],
-                            lhsT=piece[:, r, :],
-                            rhs=permutation[:],
-                            start=(n == 0),
-                            stop=(n == len(pieces) - 1),
-                            is_transpose=True,
-                        )
+        def store(s, first_row, rows):
+            in_hbm = outs[s][:, :, :, first_row : first_row + rows, :].rearrange(
+                "b (j f) g r c -> f g (b j) (r c)", f=BLOCK_HEADS
+            )
+            for f in range(BLOCK_HEADS):
+                nc.sync.dma_start(
+                    out=in_hbm[f],
+                    in_=results[s][:, f, first_row : first_row + rows, :].rearrange(
+                        "p r c -> p (r c)"
+                    ),
+                )
+
+        def turn(s, half, pieces, group_sum):
+            places = slice(HALF * half, HALF * (half + 1))
+            turned = banks.tile([P, HALF, P], F32, tag="bank")
+            for r in range(HALF):
+                for n, (piece, permutation) in enumerate(pieces):
+                    nc.tensor.matmul(
+                        out=turned[:, r, :],
+                        lhsT=piece[:, r, :],
+                        rhs=permutation[:],
+                        start=(n == 0),
+                        stop=(n == len(pieces) - 1),
+                        is_transpose=True,
+                    )
+                    if group_sum is not None:
                         nc.tensor.matmul(
                             out=group_sum[:],
                             lhsT=piece[:, r, :],
@@ -194,17 +197,79 @@ def tile_causalselfattention2_pa_s_kernel(
                             stop=(half == HALVES - 1 and r == HALF - 1 and n == len(pieces) - 1),
                             is_transpose=True,
                         )
-                nc.scalar.copy(
-                    out=result[:, :, places, :].rearrange("p f r c -> p r f c"),
-                    in_=turned[:].rearrange("p r (f c) -> p r f c", c=HEAD),
-                )
-            nc.vector.tensor_scalar_mul(
-                out=result[:, :, GROUP, :],
-                in0=group_sum[:].rearrange("p (f c) -> p f c", c=HEAD),
-                scalar1=1.0 / GROUP,
+            nc.scalar.copy(
+                out=results[s][:, :, places, :].rearrange("p f r c -> p r f c"),
+                in_=turned[:].rearrange("p r (f c) -> p r f c", c=HEAD),
             )
-            groups_of = outs[s].rearrange("b (j f) g r c -> f g (b j) (r c)", f=BLOCK_HEADS)
-            for f in range(BLOCK_HEADS):
-                nc.sync.dma_start(
-                    out=groups_of[f], in_=result[:, f, :, :].rearrange("p r c -> p (r c)")
+            return turned
+
+        k_parts = []
+        for s in range(ROTATED):
+            for half in range(HALVES):
+                places = slice(HALF * half, HALF * (half + 1))
+                pieces = []
+                for which, permutation in ((0, identity), (1, swap_pairs)):
+                    factor = (
+                        factors[:, which, places]
+                        .rearrange("p r g b -> p r (g b)")
+                        .unsqueeze(3)
+                        .to_broadcast([P, HALF, GROUPS * BATCH, HEAD_BLOCKS])
+                    )
+                    scaled = work.tile([P, HALF, P], F32, tag="scaled%d" % which)
+                    nc.vector.tensor_tensor(
+                        out=scaled[:].rearrange("p r (n j) -> p r n j", j=HEAD_BLOCKS),
+                        in0=sorted_product(s, half),
+                        in1=factor,
+                        op=MULT,
+                    )
+                    pieces.append((scaled, permutation))
+                turned = turn(s, half, pieces, None)
+                if s == 1:
+                    part = work.tile([P, P], F32, tag="part")
+                    nc.vector.tensor_reduce(
+                        out=part[:], in_=turned[:].rearrange("p r m -> p m r"), axis=AXIS_X, op=ADD
+                    )
+                    k_parts.append(part)
+            store(s, 0, GROUP)
+            result = results[s]
+            if s == 0:
+                sum4 = work.tile([P, BLOCK_HEADS, 4, HEAD], F32, tag="sum4")
+                nc.gpsimd.tensor_tensor(
+                    out=sum4[:], in0=result[:, :, 0:4, :], in1=result[:, :, 4:8, :], op=ADD
                 )
+                sum2 = work.tile([P, BLOCK_HEADS, 2, HEAD], F32, tag="sum2")
+                nc.gpsimd.tensor_tensor(
+                    out=sum2[:], in0=sum4[:, :, 0:2, :], in1=sum4[:, :, 2:4, :], op=ADD
+                )
+                sum1 = work.tile([P, BLOCK_HEADS, HEAD], F32, tag="sum1")
+                nc.gpsimd.tensor_tensor(
+                    out=sum1[:], in0=sum2[:, :, 0, :], in1=sum2[:, :, 1, :], op=ADD
+                )
+                nc.gpsimd.tensor_scalar(
+                    out=result[:, :, GROUP, :],
+                    in0=sum1[:],
+                    scalar1=1.0 / GROUP,
+                    scalar2=0.0,
+                    op0=MULT,
+                    op1=ADD,
+                )
+            else:
+                both = work.tile([P, P], F32, tag="both")
+                nc.vector.tensor_tensor(out=both[:], in0=k_parts[0][:], in1=k_parts[1][:], op=ADD)
+                nc.vector.tensor_scalar_mul(
+                    out=result[:, :, GROUP, :],
+                    in0=both[:].rearrange("p (f c) -> p f c", c=HEAD),
+                    scalar1=1.0 / GROUP,
+                )
+            store(s, GROUP, 1)
+
+        group_sum = banks.tile([P, P], F32, tag="bank")
+        turn(2, 0, [(plains[0], identity)], group_sum)
+        store(2, 0, HALF)
+        turn(2, 1, [(plains[1], identity)], group_sum)
+        nc.vector.tensor_scalar_mul(
+            out=results[2][:, :, GROUP, :],
+            in0=group_sum[:].rearrange("p (f c) -> p f c", c=HEAD),
+            scalar1=1.0 / GROUP,
+        )
+        store(2, HALF, HALF + 1)

@@ -130,7 +130,8 @@ def tile_causalselfattention2_pa_s_kernel(
             )
 
         products = {}
-        for s, half in ((0, 0), (2, 0), (2, 1), (0, 1), (1, 0), (1, 1)):
+
+        def multiply(s, half):
             tokens = slice(HALF_TOKENS * half, HALF_TOKENS * (half + 1))
             product = banks.tile([P, HEAD_BLOCKS, HALF_TOKENS], F32, tag="bank")
             for j in range(HEAD_BLOCKS):
@@ -149,14 +150,33 @@ def tile_causalselfattention2_pa_s_kernel(
         def sorted_product(s, half):
             return products[(s, half)][:].rearrange("p j (r n) -> p r n j", r=HALF)
 
-        plains = []
-        for half in range(HALVES):
+        def take_plain(half):
             plain = work.tile([P, HALF, P], F32, tag="plain")
             nc.scalar.copy(
                 out=plain[:].rearrange("p r (n j) -> p r n j", j=HEAD_BLOCKS),
                 in_=sorted_product(2, half),
             )
-            plains.append(plain)
+            return [(plain, identity)]
+
+        def rotate(s, half):
+            places = slice(HALF * half, HALF * (half + 1))
+            pieces = []
+            for which, permutation in ((0, identity), (1, swap_pairs)):
+                factor = (
+                    factors[:, which, places]
+                    .rearrange("p r g b -> p r (g b)")
+                    .unsqueeze(3)
+                    .to_broadcast([P, HALF, GROUPS * BATCH, HEAD_BLOCKS])
+                )
+                scaled = work.tile([P, HALF, P], F32, tag="scaled%d" % which)
+                nc.vector.tensor_tensor(
+                    out=scaled[:].rearrange("p r (n j) -> p r n j", j=HEAD_BLOCKS),
+                    in0=sorted_product(s, half),
+                    in1=factor,
+                    op=MULT,
+                )
+                pieces.append((scaled, permutation))
+            return pieces
 
         results = []
         for s in range(TENSORS):
@@ -176,7 +196,6 @@ def tile_causalselfattention2_pa_s_kernel(
                 )
 
         def turn(s, half, pieces, group_sum):
-            places = slice(HALF * half, HALF * (half + 1))
             turned = banks.tile([P, HALF, P], F32, tag="bank")
             for r in range(HALF):
                 for n, (piece, permutation) in enumerate(pieces):
@@ -193,83 +212,78 @@ def tile_causalselfattention2_pa_s_kernel(
                             out=group_sum[:],
                             lhsT=piece[:, r, :],
                             rhs=permutation[:],
-                            start=(half == 0 and r == 0 and n == 0),
-                            stop=(half == HALVES - 1 and r == HALF - 1 and n == len(pieces) - 1),
+                            start=(half == 0 and r == 0),
+                            stop=(half == HALVES - 1 and r == HALF - 1),
                             is_transpose=True,
                         )
+            return turned
+
+        def take_out(s, half, turned):
+            places = slice(HALF * half, HALF * (half + 1))
             nc.scalar.copy(
                 out=results[s][:, :, places, :].rearrange("p f r c -> p r f c"),
                 in_=turned[:].rearrange("p r (f c) -> p r f c", c=HEAD),
             )
-            return turned
 
-        k_parts = []
-        for s in range(ROTATED):
-            for half in range(HALVES):
-                places = slice(HALF * half, HALF * (half + 1))
-                pieces = []
-                for which, permutation in ((0, identity), (1, swap_pairs)):
-                    factor = (
-                        factors[:, which, places]
-                        .rearrange("p r g b -> p r (g b)")
-                        .unsqueeze(3)
-                        .to_broadcast([P, HALF, GROUPS * BATCH, HEAD_BLOCKS])
-                    )
-                    scaled = work.tile([P, HALF, P], F32, tag="scaled%d" % which)
-                    nc.vector.tensor_tensor(
-                        out=scaled[:].rearrange("p r (n j) -> p r n j", j=HEAD_BLOCKS),
-                        in0=sorted_product(s, half),
-                        in1=factor,
-                        op=MULT,
-                    )
-                    pieces.append((scaled, permutation))
-                turned = turn(s, half, pieces, None)
-                if s == 1:
-                    part = work.tile([P, P], F32, tag="part")
-                    nc.vector.tensor_reduce(
-                        out=part[:], in_=turned[:].rearrange("p r m -> p m r"), axis=AXIS_X, op=ADD
-                    )
-                    k_parts.append(part)
-            store(s, 0, GROUP)
-            result = results[s]
-            if s == 0:
-                sum4 = work.tile([P, BLOCK_HEADS, 4, HEAD], F32, tag="sum4")
-                nc.gpsimd.tensor_tensor(
-                    out=sum4[:], in0=result[:, :, 0:4, :], in1=result[:, :, 4:8, :], op=ADD
-                )
-                sum2 = work.tile([P, BLOCK_HEADS, 2, HEAD], F32, tag="sum2")
-                nc.gpsimd.tensor_tensor(
-                    out=sum2[:], in0=sum4[:, :, 0:2, :], in1=sum4[:, :, 2:4, :], op=ADD
-                )
-                sum1 = work.tile([P, BLOCK_HEADS, HEAD], F32, tag="sum1")
-                nc.gpsimd.tensor_tensor(
-                    out=sum1[:], in0=sum2[:, :, 0, :], in1=sum2[:, :, 1, :], op=ADD
-                )
-                nc.gpsimd.tensor_scalar(
-                    out=result[:, :, GROUP, :],
-                    in0=sum1[:],
-                    scalar1=1.0 / GROUP,
-                    scalar2=0.0,
-                    op0=MULT,
-                    op1=ADD,
-                )
-            else:
-                both = work.tile([P, P], F32, tag="both")
-                nc.vector.tensor_tensor(out=both[:], in0=k_parts[0][:], in1=k_parts[1][:], op=ADD)
-                nc.vector.tensor_scalar_mul(
-                    out=result[:, :, GROUP, :],
-                    in0=both[:].rearrange("p (f c) -> p f c", c=HEAD),
-                    scalar1=1.0 / GROUP,
-                )
-            store(s, GROUP, 1)
+        def sum_rows(turned):
+            part = work.tile([P, P], F32, tag="part")
+            nc.vector.tensor_reduce(
+                out=part[:], in_=turned[:].rearrange("p r m -> p m r"), axis=AXIS_X, op=ADD
+            )
+            return part
 
-        group_sum = banks.tile([P, P], F32, tag="bank")
-        turn(2, 0, [(plains[0], identity)], group_sum)
+        def eighth(part):
+            scaled_part = work.tile([P, P], F32, tag="scaled_part")
+            nc.scalar.mul(out=scaled_part[:], in_=part[:], mul=1.0 / GROUP)
+            return scaled_part
+
+        def mean(s, first_eighth, second_part):
+            nc.vector.scalar_tensor_tensor(
+                out=results[s][:, :, GROUP, :],
+                in0=second_part[:].rearrange("p (f c) -> p f c", c=HEAD),
+                scalar=1.0 / GROUP,
+                in1=first_eighth[:].rearrange("p (f c) -> p f c", c=HEAD),
+                op0=MULT,
+                op1=ADD,
+            )
+
+        multiply(0, 0)
+        multiply(2, 0)
+        multiply(0, 1)
+        multiply(1, 0)
+        multiply(2, 1)
+        v0_pieces = take_plain(0)
+        v1_pieces = take_plain(1)
+        q0_pieces = rotate(0, 0)
+        q1_pieces = rotate(0, 1)
+        k0_pieces = rotate(1, 0)
+        v_sum = banks.tile([P, P], F32, tag="bank")
+        v0_turned = turn(2, 0, v0_pieces, v_sum)
+        take_out(2, 0, v0_turned)
         store(2, 0, HALF)
-        turn(2, 1, [(plains[1], identity)], group_sum)
+        multiply(1, 1)
+        k1_pieces = rotate(1, 1)
+        q0_turned = turn(0, 0, q0_pieces, None)
+        take_out(0, 0, q0_turned)
+        store(0, 0, HALF)
+        q0_eighth = eighth(sum_rows(q0_turned))
+        q1_turned = turn(0, 1, q1_pieces, None)
+        take_out(0, 1, q1_turned)
+        mean(0, q0_eighth, sum_rows(q1_turned))
+        store(0, HALF, HALF + 1)
+        k0_turned = turn(1, 0, k0_pieces, None)
+        take_out(1, 0, k0_turned)
+        store(1, 0, HALF)
+        k0_eighth = eighth(sum_rows(k0_turned))
+        k1_turned = turn(1, 1, k1_pieces, None)
+        take_out(1, 1, k1_turned)
+        mean(1, k0_eighth, sum_rows(k1_turned))
+        store(1, HALF, HALF + 1)
+        v1_turned = turn(2, 1, v1_pieces, v_sum)
+        take_out(2, 1, v1_turned)
         nc.vector.tensor_scalar_mul(
             out=results[2][:, :, GROUP, :],
-            in0=group_sum[:].rearrange("p (f c) -> p f c", c=HEAD),
+            in0=v_sum[:].rearrange("p (f c) -> p f c", c=HEAD),
             scalar1=1.0 / GROUP,
         )
         store(2, HALF, HALF + 1)

@@ -44,6 +44,11 @@ def tile_causalselfattention2_pa_s_kernel(
         work = ctx.enter_context(tc.tile_pool(name="work", bufs=ROTATED * HALVES))
         banks = ctx.enter_context(tc.psum_pool(name="banks", bufs=8))
 
+        table_in = keep.tile([P, 1], F32)
+        table_out = keep.tile([P, 1], F32)
+        nc.gpsimd.memset(table_in[:], 0.0)
+        nc.scalar.copy(out=table_out[:], in_=table_in[:])
+
         cos_rows = keep.tile([P, PAIRS], BF16)
         sin_rows = keep.tile([P, PAIRS], BF16)
         nc.scalar.dma_start(out=cos_rows[:], in_=freqs_cos)
@@ -59,12 +64,7 @@ def tile_causalselfattention2_pa_s_kernel(
                 in_=w_attn_scales[0, 4 * quadrant : 4 * quadrant + 4, :].bitcast(I32),
             )
         w_words = keep.tile([P, 2 * TENSORS * CHANNELS], U8, align_bytes=64)
-        for s in (0, 2, 1):
-            tensor_bytes = slice(2 * CHANNELS * s, 2 * CHANNELS * (s + 1))
-            nc.sync.dma_start(
-                out=w_words[:, tensor_bytes].bitcast(I32),
-                in_=w_attn_words[0, :, tensor_bytes].bitcast(I32),
-            )
+        nc.sync.dma_start(out=w_words[:].bitcast(I32), in_=w_attn_words[0].bitcast(I32))
 
         identity = keep.tile([P, P], F32)
         make_identity(nc, identity[:])

@@ -234,7 +234,7 @@ def tile_causalselfattention2_pa_s_kernel(
 
         def eighth(part):
             scaled_part = work.tile([P, P], F32, tag="scaled_part")
-            nc.scalar.mul(out=scaled_part[:], in_=part[:], mul=1.0 / GROUP)
+            nc.vector.tensor_scalar_mul(out=scaled_part[:], in0=part[:], scalar1=1.0 / GROUP)
             return scaled_part
 
         def mean(s, first_eighth, second_part):
@@ -269,21 +269,21 @@ def tile_causalselfattention2_pa_s_kernel(
         q0_eighth = eighth(sum_rows(q0_turned))
         q1_turned = turn(0, 1, q1_pieces, None)
         take_out(0, 1, q1_turned)
-        mean(0, q0_eighth, sum_rows(q1_turned))
-        store(0, HALF, HALF + 1)
         k0_turned = turn(1, 0, k0_pieces, None)
         take_out(1, 0, k0_turned)
         store(1, 0, HALF)
+        mean(0, q0_eighth, sum_rows(q1_turned))
+        store(0, HALF, HALF + 1)
         k0_eighth = eighth(sum_rows(k0_turned))
         k1_turned = turn(1, 1, k1_pieces, None)
         take_out(1, 1, k1_turned)
-        mean(1, k0_eighth, sum_rows(k1_turned))
-        store(1, HALF, HALF + 1)
         v1_turned = turn(2, 1, v1_pieces, v_sum)
         take_out(2, 1, v1_turned)
-        nc.vector.tensor_scalar_mul(
+        nc.scalar.mul(
             out=results[2][:, :, GROUP, :],
-            in0=v_sum[:].rearrange("p (f c) -> p f c", c=HEAD),
-            scalar1=1.0 / GROUP,
+            in_=v_sum[:].rearrange("p (f c) -> p f c", c=HEAD),
+            mul=1.0 / GROUP,
         )
         store(2, HALF, HALF + 1)
+        mean(1, k0_eighth, sum_rows(k1_turned))
+        store(1, HALF, HALF + 1)

@@ -30,6 +30,7 @@ HALVES = 2
 HALF = GROUP // HALVES
 TOKENS = BATCH * POSITIONS
 HALF_TOKENS = TOKENS // HALVES
+assert HALF_TOKENS == P
 
 FLOPS = 2 * TOKENS * CHANNELS * TENSORS * CHANNELS
 
@@ -43,18 +44,25 @@ def tile_causalselfattention2_pa_s_kernel(
         keep = ctx.enter_context(tc.tile_pool(name="keep", bufs=1))
         work = ctx.enter_context(tc.tile_pool(name="work", bufs=ROTATED * HALVES))
         banks = ctx.enter_context(tc.psum_pool(name="banks", bufs=8))
+        ctx.enter_context(tc.manual_schedule())
+
+        cos_rows = keep.tile([P, PAIRS], BF16)
+        sin_rows = keep.tile([P, PAIRS], BF16)
+        x_halves_in_hbm = x.rearrange("b (g h r) c -> h (b g) r c", g=GROUPS, h=HALVES)
+        x_rows = []
+        for half in range(HALVES):
+            x_half = keep.tile([P, CHANNELS], BF16, name="x_half%d" % half)
+            x_rows.append(x_half)
+        nc.sync.dma_start(out=x_rows[0][:], in_=x_halves_in_hbm[0])
+        nc.scalar.dma_start(out=cos_rows[:], in_=freqs_cos)
+        nc.sync.dma_start(out=sin_rows[:], in_=freqs_sin)
+        w_words = keep.tile([P, 2 * TENSORS * CHANNELS], U8, align_bytes=64)
+        nc.sync.dma_start(out=w_words[:].bitcast(I32), in_=w_attn_words[0].bitcast(I32))
 
         table_in = keep.tile([P, 1], F32)
         table_out = keep.tile([P, 1], F32)
         nc.gpsimd.memset(table_in[:], 0.0)
         nc.scalar.copy(out=table_out[:], in_=table_in[:])
-
-        cos_rows = keep.tile([P, PAIRS], BF16)
-        sin_rows = keep.tile([P, PAIRS], BF16)
-        nc.scalar.dma_start(out=cos_rows[:], in_=freqs_cos)
-        nc.scalar.dma_start(out=sin_rows[:], in_=freqs_sin)
-        x_rows = keep.tile([P, BATCH, CHANNELS], BF16)
-        nc.sync.dma_start(out=x_rows[:], in_=x.rearrange("b t c -> t b c"))
 
         w_scales = keep.tile([P, TENSORS * CHANNELS], U8, align_bytes=64)
         nc.vector.memset(w_scales[:].bitcast(I32), 0)
@@ -63,16 +71,20 @@ def tile_causalselfattention2_pa_s_kernel(
                 out=w_scales[32 * quadrant : 32 * quadrant + 4, :].bitcast(I32),
                 in_=w_attn_scales[0, 4 * quadrant : 4 * quadrant + 4, :].bitcast(I32),
             )
-        w_words = keep.tile([P, 2 * TENSORS * CHANNELS], U8, align_bytes=64)
-        nc.sync.dma_start(out=w_words[:].bitcast(I32), in_=w_attn_words[0].bitcast(I32))
 
         identity = keep.tile([P, P], F32)
         make_identity(nc, identity[:])
+        nc.gpsimd.dma_start(out=x_rows[1][:], in_=x_halves_in_hbm[1])
         swap_pairs = keep.tile([P, P], F32)
         identity_pairs = identity[:].rearrange("p (m e) -> p m e", e=2)
         swapped_pairs = swap_pairs[:].rearrange("p (m e) -> p m e", e=2)
-        nc.gpsimd.tensor_copy(out=swapped_pairs[:, :, 0], in_=identity_pairs[:, :, 1])
-        nc.gpsimd.tensor_copy(out=swapped_pairs[:, :, 1], in_=identity_pairs[:, :, 0])
+        sort_half = keep.tile([P, P], F32)
+        nc.vector.tensor_copy(
+            out=sort_half[:].rearrange("p (r g b) -> p r g b", r=HALF, g=GROUPS),
+            in_=identity[:].rearrange("p (b g r) -> p r g b", b=BATCH, g=GROUPS),
+        )
+        nc.vector.tensor_copy(out=swapped_pairs[:, :, 0], in_=identity_pairs[:, :, 1])
+        nc.vector.tensor_copy(out=swapped_pairs[:, :, 1], in_=identity_pairs[:, :, 0])
 
         cos_wide = keep.tile([P, BLOCK_HEADS, PAIRS, 2], F32)
         sin_wide = keep.tile([P, BLOCK_HEADS, PAIRS, 2], F32)
@@ -84,13 +96,42 @@ def tile_causalselfattention2_pa_s_kernel(
         nc.vector.tensor_copy(out=sin_wide[:, :, :, 0], in_=sin_heads)
         nc.vector.tensor_scalar_mul(out=sin_wide[:, :, :, 1], in0=sin_heads, scalar1=-1.0)
 
-        x_words = x_rows[:].bitcast(F32)
-        x_bank = banks.tile([P, BATCH, 2, POSITIONS], F32, tag="bank")
-        for b in range(BATCH):
+        x_grouped = keep.tile([P, TOKENS, 4], BF16, align_bytes=64)
+        x_grouped_words = (
+            x_grouped[:]
+            .rearrange("p n t -> p (n t)")
+            .bitcast(F32)
+            .rearrange("p (n u) -> p n u", u=2)
+        )
+        x_codes = keep.tile([P, TOKENS], U32, align_bytes=64)
+        x_scales = keep.tile([P, TOKENS], U8, align_bytes=64)
+
+        def half_tokens(half):
+            return slice(HALF_TOKENS * half, HALF_TOKENS * (half + 1))
+
+        def turn_x(half):
+            x_bank = banks.tile([P, 2, HALF_TOKENS], F32, tag="bank")
+            words = x_rows[half][:].bitcast(F32)
             for u in range(2):
-                nc.tensor.transpose(
-                    x_bank[:, b, u, :], x_words[:, b, u : CHANNELS // 2 : 2], identity[:]
+                nc.tensor.matmul(
+                    out=x_bank[:, u, :],
+                    lhsT=words[:, u : CHANNELS // 2 : 2],
+                    rhs=sort_half[:],
+                    start=True,
+                    stop=True,
+                    is_transpose=True,
                 )
+            return x_bank
+
+        def quantize_x(half):
+            tokens = half_tokens(half)
+            nc.vector.quantize_mx(
+                out=x_codes[:, tokens].bitcast(FP8X4),
+                scales=x_scales[:, tokens],
+                in_=x_grouped[:, tokens, :].rearrange("p n t -> p (n t)"),
+            )
+
+        x0_bank = turn_x(0)
         factors_bank = banks.tile([P, 2, POSITIONS], F32, tag="bank")
         nc.tensor.transpose(
             factors_bank[:, 0, :], cos_wide[:].rearrange("p f i e -> p (f i e)"), identity[:]
@@ -98,26 +139,10 @@ def tile_causalselfattention2_pa_s_kernel(
         nc.tensor.transpose(
             factors_bank[:, 1, :], sin_wide[:].rearrange("p f i e -> p (f i e)"), identity[:]
         )
-
-        x_grouped = keep.tile([P, TOKENS, 4], BF16, align_bytes=64)
-        x_grouped_words = (
-            x_grouped[:]
-            .rearrange("p n t -> p (n t)")
-            .bitcast(F32)
-            .rearrange("p (r g b u) -> p r g b u", r=GROUP, g=GROUPS, b=BATCH)
+        nc.vector.tensor_copy(
+            out=x_grouped_words[:, half_tokens(0)], in_=x0_bank[:].rearrange("p u n -> p n u")
         )
-        x_bank_sorted = x_bank[:].rearrange("p b u (g r) -> p r g b u", r=GROUP)
-        x_codes = keep.tile([P, TOKENS], U32, align_bytes=64)
-        x_scales = keep.tile([P, TOKENS], U8, align_bytes=64)
-        nc.vector.tensor_copy(out=x_grouped_words[:, 0:HALF], in_=x_bank_sorted[:, 0:HALF])
-        nc.scalar.copy(out=x_grouped_words[:, HALF:GROUP], in_=x_bank_sorted[:, HALF:GROUP])
-        for half in range(HALVES):
-            tokens = slice(HALF_TOKENS * half, HALF_TOKENS * (half + 1))
-            nc.vector.quantize_mx(
-                out=x_codes[:, tokens].bitcast(FP8X4),
-                scales=x_scales[:, tokens],
-                in_=x_grouped[:, tokens, :].rearrange("p n t -> p (n t)"),
-            )
+        quantize_x(0)
 
         factors = keep.tile([P, 2, GROUP, GROUPS, BATCH], F32)
         for which in range(2):
@@ -132,7 +157,7 @@ def tile_causalselfattention2_pa_s_kernel(
         products = {}
 
         def multiply(s, half):
-            tokens = slice(HALF_TOKENS * half, HALF_TOKENS * (half + 1))
+            tokens = half_tokens(half)
             product = banks.tile([P, HEAD_BLOCKS, HALF_TOKENS], F32, tag="bank")
             for j in range(HEAD_BLOCKS):
                 first = CHANNELS * s + P * j
@@ -184,18 +209,16 @@ def tile_causalselfattention2_pa_s_kernel(
             results.append(result)
 
         def store(s, first_row, rows):
-            in_hbm = outs[s][:, :, :, first_row : first_row + rows, :].rearrange(
-                "b (j f) g r c -> f g (b j) (r c)", f=BLOCK_HEADS
+            nc.sync.dma_start(
+                out=outs[s][:, :, :, first_row : first_row + rows, :].rearrange(
+                    "b h g r c -> g (b h) (r c)"
+                ),
+                in_=results[s][:, :, first_row : first_row + rows, :].rearrange(
+                    "p f r c -> p f (r c)"
+                ),
             )
-            for f in range(BLOCK_HEADS):
-                nc.sync.dma_start(
-                    out=in_hbm[f],
-                    in_=results[s][:, f, first_row : first_row + rows, :].rearrange(
-                        "p r c -> p (r c)"
-                    ),
-                )
 
-        def turn(s, half, pieces, group_sum):
+        def turn(pieces):
             turned = banks.tile([P, HALF, P], F32, tag="bank")
             for r in range(HALF):
                 for n, (piece, permutation) in enumerate(pieces):
@@ -207,16 +230,21 @@ def tile_causalselfattention2_pa_s_kernel(
                         stop=(n == len(pieces) - 1),
                         is_transpose=True,
                     )
-                    if group_sum is not None:
-                        nc.tensor.matmul(
-                            out=group_sum[:],
-                            lhsT=piece[:, r, :],
-                            rhs=permutation[:],
-                            start=(half == 0 and r == 0),
-                            stop=(half == HALVES - 1 and r == HALF - 1),
-                            is_transpose=True,
-                        )
             return turned
+
+        def turn_and_add(pieces):
+            added = banks.tile([P, P], F32, tag="bank")
+            steps = [(piece, r, permutation) for piece, permutation in pieces for r in range(HALF)]
+            for n, (piece, r, permutation) in enumerate(steps):
+                nc.tensor.matmul(
+                    out=added[:],
+                    lhsT=piece[:, r, :],
+                    rhs=permutation[:],
+                    start=(n == 0),
+                    stop=(n == len(steps) - 1),
+                    is_transpose=True,
+                )
+            return added
 
         def take_out(s, half, turned):
             places = slice(HALF * half, HALF * (half + 1))
@@ -231,6 +259,15 @@ def tile_causalselfattention2_pa_s_kernel(
                 out=part[:], in_=turned[:].rearrange("p r m -> p m r"), axis=AXIS_X, op=ADD
             )
             return part
+
+        def add_plain(plain):
+            pairs = work.tile([P, 2, P], F32, tag="pairs")
+            nc.gpsimd.tensor_tensor(
+                out=pairs[:], in0=plain[:, 0:2, :], in1=plain[:, 2:4, :], op=ADD
+            )
+            four = work.tile([P, P], F32, tag="four")
+            nc.gpsimd.tensor_tensor(out=four[:], in0=pairs[:, 0, :], in1=pairs[:, 1, :], op=ADD)
+            return four
 
         def eighth(part):
             scaled_part = work.tile([P, P], F32, tag="scaled_part")
@@ -248,42 +285,56 @@ def tile_causalselfattention2_pa_s_kernel(
             )
 
         multiply(0, 0)
-        multiply(2, 0)
-        multiply(0, 1)
+        x1_bank = turn_x(1)
+        nc.scalar.copy(
+            out=x_grouped_words[:, half_tokens(1)], in_=x1_bank[:].rearrange("p u n -> p n u")
+        )
         multiply(1, 0)
-        multiply(2, 1)
-        v0_pieces = take_plain(0)
-        v1_pieces = take_plain(1)
+        multiply(2, 0)
         q0_pieces = rotate(0, 0)
-        q1_pieces = rotate(0, 1)
+        quantize_x(1)
         k0_pieces = rotate(1, 0)
-        v_sum = banks.tile([P, P], F32, tag="bank")
-        v0_turned = turn(2, 0, v0_pieces, v_sum)
-        take_out(2, 0, v0_turned)
-        store(2, 0, HALF)
-        multiply(1, 1)
-        k1_pieces = rotate(1, 1)
-        q0_turned = turn(0, 0, q0_pieces, None)
+        v0_pieces = take_plain(0)
+        v0_added = add_plain(v0_pieces[0][0])
+        multiply(0, 1)
+        q1_pieces = rotate(0, 1)
+        q0_turned = turn(q0_pieces)
         take_out(0, 0, q0_turned)
         store(0, 0, HALF)
-        q0_eighth = eighth(sum_rows(q0_turned))
-        q1_turned = turn(0, 1, q1_pieces, None)
-        take_out(0, 1, q1_turned)
-        k0_turned = turn(1, 0, k0_pieces, None)
+        multiply(1, 1)
+        k1_pieces = rotate(1, 1)
+        v0_turned = turn(v0_pieces)
+        take_out(2, 0, v0_turned)
+        store(2, 0, HALF)
+        multiply(2, 1)
+        v1_pieces = take_plain(1)
+        v1_added = add_plain(v1_pieces[0][0])
+        v_added = work.tile([P, P], F32, tag="v_added")
+        nc.gpsimd.tensor_tensor(out=v_added[:], in0=v0_added[:], in1=v1_added[:], op=ADD)
+        k0_turned = turn(k0_pieces)
         take_out(1, 0, k0_turned)
         store(1, 0, HALF)
-        mean(0, q0_eighth, sum_rows(q1_turned))
-        store(0, HALF, HALF + 1)
+        q0_eighth = eighth(sum_rows(q0_turned))
         k0_eighth = eighth(sum_rows(k0_turned))
-        k1_turned = turn(1, 1, k1_pieces, None)
+        q1_turned = turn(q1_pieces)
+        take_out(0, 1, q1_turned)
+        store(0, HALF, HALF)
+        mean(0, q0_eighth, sum_rows(q1_turned))
+        k1_turned = turn(k1_pieces)
         take_out(1, 1, k1_turned)
-        v1_turned = turn(2, 1, v1_pieces, v_sum)
+        store(1, HALF, HALF)
+        v1_turned = turn(v1_pieces)
         take_out(2, 1, v1_turned)
+        store(2, HALF, HALF)
+        k1_added = turn_and_add(k1_pieces)
+        mean(1, k0_eighth, k1_added)
+        v_sum = banks.tile([P, P], F32, tag="bank")
+        nc.tensor.transpose(v_sum[:], v_added[:], identity[:])
         nc.scalar.mul(
             out=results[2][:, :, GROUP, :],
             in_=v_sum[:].rearrange("p (f c) -> p f c", c=HEAD),
             mul=1.0 / GROUP,
         )
-        store(2, HALF, HALF + 1)
-        mean(1, k0_eighth, sum_rows(k1_turned))
-        store(1, HALF, HALF + 1)
+        store(0, GROUP, 1)
+        store(1, GROUP, 1)
+        store(2, GROUP, 1)

@@ -71,10 +71,10 @@ def tile_causalselfattention2_pa_s_kernel(
                 out=w_scales[32 * quadrant : 32 * quadrant + 4, :].bitcast(I32),
                 in_=w_attn_scales[0, 4 * quadrant : 4 * quadrant + 4, :].bitcast(I32),
             )
+        nc.sync.dma_start(out=x_rows[1][:], in_=x_halves_in_hbm[1])
 
         identity = keep.tile([P, P], F32)
         make_identity(nc, identity[:])
-        nc.gpsimd.dma_start(out=x_rows[1][:], in_=x_halves_in_hbm[1])
         swap_pairs = keep.tile([P, P], F32)
         identity_pairs = identity[:].rearrange("p (m e) -> p m e", e=2)
         swapped_pairs = swap_pairs[:].rearrange("p (m e) -> p m e", e=2)
@@ -285,11 +285,11 @@ def tile_causalselfattention2_pa_s_kernel(
             )
 
         multiply(0, 0)
+        multiply(1, 0)
         x1_bank = turn_x(1)
         nc.scalar.copy(
             out=x_grouped_words[:, half_tokens(1)], in_=x1_bank[:].rearrange("p u n -> p n u")
         )
-        multiply(1, 0)
         multiply(2, 0)
         q0_pieces = rotate(0, 0)
         quantize_x(1)
@@ -298,17 +298,17 @@ def tile_causalselfattention2_pa_s_kernel(
         v0_added = add_plain(v0_pieces[0][0])
         multiply(0, 1)
         q1_pieces = rotate(0, 1)
-        q0_turned = turn(q0_pieces)
-        take_out(0, 0, q0_turned)
-        store(0, 0, HALF)
-        multiply(1, 1)
-        k1_pieces = rotate(1, 1)
-        v0_turned = turn(v0_pieces)
-        take_out(2, 0, v0_turned)
-        store(2, 0, HALF)
         multiply(2, 1)
         v1_pieces = take_plain(1)
         v1_added = add_plain(v1_pieces[0][0])
+        multiply(1, 1)
+        k1_pieces = rotate(1, 1)
+        q0_turned = turn(q0_pieces)
+        take_out(0, 0, q0_turned)
+        store(0, 0, HALF)
+        v0_turned = turn(v0_pieces)
+        take_out(2, 0, v0_turned)
+        store(2, 0, HALF)
         v_added = work.tile([P, P], F32, tag="v_added")
         nc.gpsimd.tensor_tensor(out=v_added[:], in0=v0_added[:], in1=v1_added[:], op=ADD)
         k0_turned = turn(k0_pieces)
@@ -320,21 +320,20 @@ def tile_causalselfattention2_pa_s_kernel(
         take_out(0, 1, q1_turned)
         store(0, HALF, HALF)
         mean(0, q0_eighth, sum_rows(q1_turned))
-        k1_turned = turn(k1_pieces)
-        take_out(1, 1, k1_turned)
-        store(1, HALF, HALF)
         v1_turned = turn(v1_pieces)
-        take_out(2, 1, v1_turned)
-        store(2, HALF, HALF)
-        k1_added = turn_and_add(k1_pieces)
-        mean(1, k0_eighth, k1_added)
         v_sum = banks.tile([P, P], F32, tag="bank")
         nc.tensor.transpose(v_sum[:], v_added[:], identity[:])
+        take_out(2, 1, v1_turned)
         nc.scalar.mul(
             out=results[2][:, :, GROUP, :],
             in_=v_sum[:].rearrange("p (f c) -> p f c", c=HEAD),
             mul=1.0 / GROUP,
         )
+        store(2, HALF, HALF + 1)
         store(0, GROUP, 1)
+        k1_turned = turn(k1_pieces)
+        take_out(1, 1, k1_turned)
+        store(1, HALF, HALF)
+        k1_added = turn_and_add(k1_pieces)
+        mean(1, k0_eighth, k1_added)
         store(1, GROUP, 1)
-        store(2, GROUP, 1)

@@ -56,8 +56,6 @@ def tile_causalselfattention2_pa_s_kernel(
         nc.sync.dma_start(out=x_rows[0][:], in_=x_halves_in_hbm[0])
         nc.scalar.dma_start(out=cos_rows[:], in_=freqs_cos)
         nc.sync.dma_start(out=sin_rows[:], in_=freqs_sin)
-        w_words = keep.tile([P, 2 * TENSORS * CHANNELS], U8, align_bytes=64)
-        nc.sync.dma_start(out=w_words[:].bitcast(I32), in_=w_attn_words[0].bitcast(I32))
 
         table_in = keep.tile([P, 1], F32)
         table_out = keep.tile([P, 1], F32)
@@ -71,6 +69,8 @@ def tile_causalselfattention2_pa_s_kernel(
                 out=w_scales[32 * quadrant : 32 * quadrant + 4, :].bitcast(I32),
                 in_=w_attn_scales[0, 4 * quadrant : 4 * quadrant + 4, :].bitcast(I32),
             )
+        w_words = keep.tile([P, 2 * TENSORS * CHANNELS], U8, align_bytes=64)
+        nc.sync.dma_start(out=w_words[:].bitcast(I32), in_=w_attn_words[0].bitcast(I32))
         nc.sync.dma_start(out=x_rows[1][:], in_=x_halves_in_hbm[1])
 
         identity = keep.tile([P, P], F32)

@@ -48,14 +48,15 @@ def tile_causalselfattention2_pa_s_kernel(
 
         cos_rows = keep.tile([P, PAIRS], BF16)
         sin_rows = keep.tile([P, PAIRS], BF16)
-        x_halves_in_hbm = x.rearrange("b (g h r) c -> h (b g) r c", g=GROUPS, h=HALVES)
-        x_rows = []
-        for half in range(HALVES):
-            x_half = keep.tile([P, CHANNELS], BF16, name="x_half%d" % half)
-            x_rows.append(x_half)
-        nc.sync.dma_start(out=x_rows[0][:], in_=x_halves_in_hbm[0])
         nc.scalar.dma_start(out=cos_rows[:], in_=freqs_cos)
         nc.sync.dma_start(out=sin_rows[:], in_=freqs_sin)
+        x_rows = keep.tile([P, 2, CHANNELS], BF16)
+        nc.sync.dma_start(
+            out=x_rows[:].rearrange("p e k -> p (e k)"),
+            in_=x.rearrange("b (q e) k -> (b q) (e k)", e=2),
+        )
+        w_words = keep.tile([P, 2 * TENSORS * CHANNELS], U8, align_bytes=64)
+        nc.sync.dma_start(out=w_words[:].bitcast(I32), in_=w_attn_words[0].bitcast(I32))
 
         table_in = keep.tile([P, 1], F32)
         table_out = keep.tile([P, 1], F32)
@@ -69,32 +70,19 @@ def tile_causalselfattention2_pa_s_kernel(
                 out=w_scales[32 * quadrant : 32 * quadrant + 4, :].bitcast(I32),
                 in_=w_attn_scales[0, 4 * quadrant : 4 * quadrant + 4, :].bitcast(I32),
             )
-        w_words = keep.tile([P, 2 * TENSORS * CHANNELS], U8, align_bytes=64)
-        nc.sync.dma_start(out=w_words[:].bitcast(I32), in_=w_attn_words[0].bitcast(I32))
-        nc.sync.dma_start(out=x_rows[1][:], in_=x_halves_in_hbm[1])
 
         identity = keep.tile([P, P], F32)
         make_identity(nc, identity[:])
         swap_pairs = keep.tile([P, P], F32)
         identity_pairs = identity[:].rearrange("p (m e) -> p m e", e=2)
         swapped_pairs = swap_pairs[:].rearrange("p (m e) -> p m e", e=2)
-        sort_half = keep.tile([P, P], F32)
+        sort_tokens = keep.tile([P, P], F32)
         nc.vector.tensor_copy(
-            out=sort_half[:].rearrange("p (r g b) -> p r g b", r=HALF, g=GROUPS),
-            in_=identity[:].rearrange("p (b g r) -> p r g b", b=BATCH, g=GROUPS),
+            out=sort_tokens[:].rearrange("p (d g b) -> p d g b", d=HALF, g=GROUPS),
+            in_=identity[:].rearrange("p (b g d) -> p d g b", b=BATCH, g=GROUPS),
         )
         nc.vector.tensor_copy(out=swapped_pairs[:, :, 0], in_=identity_pairs[:, :, 1])
         nc.vector.tensor_copy(out=swapped_pairs[:, :, 1], in_=identity_pairs[:, :, 0])
-
-        cos_wide = keep.tile([P, BLOCK_HEADS, PAIRS, 2], F32)
-        sin_wide = keep.tile([P, BLOCK_HEADS, PAIRS, 2], F32)
-        nc.vector.tensor_copy(
-            out=cos_wide[:],
-            in_=cos_rows[:].unsqueeze(1).unsqueeze(3).to_broadcast([P, BLOCK_HEADS, PAIRS, 2]),
-        )
-        sin_heads = sin_rows[:].unsqueeze(1).to_broadcast([P, BLOCK_HEADS, PAIRS])
-        nc.vector.tensor_copy(out=sin_wide[:, :, :, 0], in_=sin_heads)
-        nc.vector.tensor_scalar_mul(out=sin_wide[:, :, :, 1], in0=sin_heads, scalar1=-1.0)
 
         x_grouped = keep.tile([P, TOKENS, 4], BF16, align_bytes=64)
         x_grouped_words = (
@@ -106,46 +94,42 @@ def tile_causalselfattention2_pa_s_kernel(
         x_codes = keep.tile([P, TOKENS], U32, align_bytes=64)
         x_scales = keep.tile([P, TOKENS], U8, align_bytes=64)
 
-        def half_tokens(half):
-            return slice(HALF_TOKENS * half, HALF_TOKENS * (half + 1))
+        def parity_tokens(e):
+            return slice(HALF_TOKENS * e, HALF_TOKENS * (e + 1))
 
-        def turn_x(half):
+        def turn_x(e):
             x_bank = banks.tile([P, 2, HALF_TOKENS], F32, tag="bank")
-            words = x_rows[half][:].bitcast(F32)
+            words = x_rows[:, e, :].bitcast(F32)
             for u in range(2):
                 nc.tensor.matmul(
                     out=x_bank[:, u, :],
                     lhsT=words[:, u : CHANNELS // 2 : 2],
-                    rhs=sort_half[:],
+                    rhs=sort_tokens[:],
                     start=True,
                     stop=True,
                     is_transpose=True,
                 )
             return x_bank
 
-        def quantize_x(half):
-            tokens = half_tokens(half)
+        def quantize_x(e):
+            tokens = parity_tokens(e)
             nc.vector.quantize_mx(
                 out=x_codes[:, tokens].bitcast(FP8X4),
                 scales=x_scales[:, tokens],
                 in_=x_grouped[:, tokens, :].rearrange("p n t -> p (n t)"),
             )
 
-        x0_bank = turn_x(0)
+        cos_wide = keep.tile([P, BLOCK_HEADS, PAIRS, 2], F32)
+        sin_wide = keep.tile([P, BLOCK_HEADS, PAIRS, 2], F32)
         factors_bank = banks.tile([P, 2, POSITIONS], F32, tag="bank")
-        nc.tensor.transpose(
-            factors_bank[:, 0, :], cos_wide[:].rearrange("p f i e -> p (f i e)"), identity[:]
-        )
-        nc.tensor.transpose(
-            factors_bank[:, 1, :], sin_wide[:].rearrange("p f i e -> p (f i e)"), identity[:]
-        )
-        nc.vector.tensor_copy(
-            out=x_grouped_words[:, half_tokens(0)], in_=x0_bank[:].rearrange("p u n -> p n u")
-        )
-        quantize_x(0)
-
         factors = keep.tile([P, 2, GROUP, GROUPS, BATCH], F32)
-        for which in range(2):
+
+        def turn_factor(which, wide):
+            nc.tensor.transpose(
+                factors_bank[:, which, :], wide[:].rearrange("p f i e -> p (f i e)"), identity[:]
+            )
+
+        def spread_factor(which):
             nc.scalar.copy(
                 out=factors[:, which],
                 in_=factors_bank[:, which, :]
@@ -154,10 +138,34 @@ def tile_causalselfattention2_pa_s_kernel(
                 .to_broadcast([P, GROUP, GROUPS, BATCH]),
             )
 
+        nc.vector.tensor_copy(
+            out=cos_wide[:],
+            in_=cos_rows[:].unsqueeze(1).unsqueeze(3).to_broadcast([P, BLOCK_HEADS, PAIRS, 2]),
+        )
+        sin_heads = sin_rows[:].unsqueeze(1).to_broadcast([P, BLOCK_HEADS, PAIRS])
+        nc.vector.tensor_copy(out=sin_wide[:, :, :, 0], in_=sin_heads)
+        nc.vector.tensor_scalar_mul(out=sin_wide[:, :, :, 1], in0=sin_heads, scalar1=-1.0)
+        x_even_bank = turn_x(0)
+        x_odd_bank = turn_x(1)
+        turn_factor(0, cos_wide)
+        turn_factor(1, sin_wide)
+        nc.vector.tensor_copy(
+            out=x_grouped_words[:, parity_tokens(0)],
+            in_=x_even_bank[:].rearrange("p u n -> p n u"),
+        )
+        nc.scalar.copy(
+            out=x_grouped_words[:, parity_tokens(1)],
+            in_=x_odd_bank[:].rearrange("p u n -> p n u"),
+        )
+        quantize_x(0)
+        quantize_x(1)
+        spread_factor(0)
+        spread_factor(1)
+
         products = {}
 
-        def multiply(s, half):
-            tokens = half_tokens(half)
+        def multiply(s, e):
+            tokens = parity_tokens(e)
             product = banks.tile([P, HEAD_BLOCKS, HALF_TOKENS], F32, tag="bank")
             for j in range(HEAD_BLOCKS):
                 first = CHANNELS * s + P * j
@@ -170,33 +178,32 @@ def tile_causalselfattention2_pa_s_kernel(
                     start=True,
                     stop=True,
                 )
-            products[(s, half)] = product
+            products[(s, e)] = product
 
-        def sorted_product(s, half):
-            return products[(s, half)][:].rearrange("p j (r n) -> p r n j", r=HALF)
+        def sorted_product(s, e):
+            return products[(s, e)][:].rearrange("p j (d n) -> p d n j", d=HALF)
 
-        def take_plain(half):
+        def take_plain(e):
             plain = work.tile([P, HALF, P], F32, tag="plain")
             nc.scalar.copy(
-                out=plain[:].rearrange("p r (n j) -> p r n j", j=HEAD_BLOCKS),
-                in_=sorted_product(2, half),
+                out=plain[:].rearrange("p d (n j) -> p d n j", j=HEAD_BLOCKS),
+                in_=sorted_product(2, e),
             )
             return [(plain, identity)]
 
-        def rotate(s, half):
-            places = slice(HALF * half, HALF * (half + 1))
+        def rotate(s, e):
             pieces = []
             for which, permutation in ((0, identity), (1, swap_pairs)):
                 factor = (
-                    factors[:, which, places]
-                    .rearrange("p r g b -> p r (g b)")
+                    factors[:, which, e:GROUP:2]
+                    .rearrange("p d g b -> p d (g b)")
                     .unsqueeze(3)
                     .to_broadcast([P, HALF, GROUPS * BATCH, HEAD_BLOCKS])
                 )
                 scaled = work.tile([P, HALF, P], F32, tag="scaled%d" % which)
                 nc.vector.tensor_tensor(
-                    out=scaled[:].rearrange("p r (n j) -> p r n j", j=HEAD_BLOCKS),
-                    in0=sorted_product(s, half),
+                    out=scaled[:].rearrange("p d (n j) -> p d n j", j=HEAD_BLOCKS),
+                    in0=sorted_product(s, e),
                     in1=factor,
                     op=MULT,
                 )
@@ -218,47 +225,32 @@ def tile_causalselfattention2_pa_s_kernel(
                 ),
             )
 
+        def transpose_into(out, piece, permutation, start, stop):
+            nc.tensor.matmul(
+                out=out, lhsT=piece, rhs=permutation[:], start=start, stop=stop, is_transpose=True
+            )
+
         def turn(pieces):
             turned = banks.tile([P, HALF, P], F32, tag="bank")
-            for r in range(HALF):
+            for d in range(HALF):
                 for n, (piece, permutation) in enumerate(pieces):
-                    nc.tensor.matmul(
-                        out=turned[:, r, :],
-                        lhsT=piece[:, r, :],
-                        rhs=permutation[:],
-                        start=(n == 0),
-                        stop=(n == len(pieces) - 1),
-                        is_transpose=True,
+                    transpose_into(
+                        turned[:, d, :], piece[:, d, :], permutation, n == 0, n == len(pieces) - 1
                     )
             return turned
 
         def turn_and_add(pieces):
             added = banks.tile([P, P], F32, tag="bank")
-            steps = [(piece, r, permutation) for piece, permutation in pieces for r in range(HALF)]
-            for n, (piece, r, permutation) in enumerate(steps):
-                nc.tensor.matmul(
-                    out=added[:],
-                    lhsT=piece[:, r, :],
-                    rhs=permutation[:],
-                    start=(n == 0),
-                    stop=(n == len(steps) - 1),
-                    is_transpose=True,
-                )
+            steps = [(piece, d, permutation) for d in range(HALF) for piece, permutation in pieces]
+            for n, (piece, d, permutation) in enumerate(steps):
+                transpose_into(added[:], piece[:, d, :], permutation, n == 0, n == len(steps) - 1)
             return added
 
-        def take_out(s, half, turned):
-            places = slice(HALF * half, HALF * (half + 1))
+        def take_out(s, e, turned):
             nc.scalar.copy(
-                out=results[s][:, :, places, :].rearrange("p f r c -> p r f c"),
+                out=results[s][:, :, e:GROUP:2, :].rearrange("p f r c -> p r f c"),
                 in_=turned[:].rearrange("p r (f c) -> p r f c", c=HEAD),
             )
-
-        def sum_rows(turned):
-            part = work.tile([P, P], F32, tag="part")
-            nc.vector.tensor_reduce(
-                out=part[:], in_=turned[:].rearrange("p r m -> p m r"), axis=AXIS_X, op=ADD
-            )
-            return part
 
         def add_plain(plain):
             pairs = work.tile([P, 2, P], F32, tag="pairs")
@@ -268,6 +260,13 @@ def tile_causalselfattention2_pa_s_kernel(
             four = work.tile([P, P], F32, tag="four")
             nc.gpsimd.tensor_tensor(out=four[:], in0=pairs[:, 0, :], in1=pairs[:, 1, :], op=ADD)
             return four
+
+        def sum_rows(turned):
+            part = work.tile([P, P], F32, tag="part")
+            nc.vector.tensor_reduce(
+                out=part[:], in_=turned[:].rearrange("p r m -> p m r"), axis=AXIS_X, op=ADD
+            )
+            return part
 
         def eighth(part):
             scaled_part = work.tile([P, P], F32, tag="scaled_part")
@@ -285,55 +284,51 @@ def tile_causalselfattention2_pa_s_kernel(
             )
 
         multiply(0, 0)
-        multiply(1, 0)
-        x1_bank = turn_x(1)
-        nc.scalar.copy(
-            out=x_grouped_words[:, half_tokens(1)], in_=x1_bank[:].rearrange("p u n -> p n u")
-        )
-        multiply(2, 0)
-        q0_pieces = rotate(0, 0)
-        quantize_x(1)
-        k0_pieces = rotate(1, 0)
-        v0_pieces = take_plain(0)
-        v0_added = add_plain(v0_pieces[0][0])
         multiply(0, 1)
-        q1_pieces = rotate(0, 1)
+        multiply(2, 0)
         multiply(2, 1)
-        v1_pieces = take_plain(1)
-        v1_added = add_plain(v1_pieces[0][0])
+        multiply(1, 0)
         multiply(1, 1)
-        k1_pieces = rotate(1, 1)
-        q0_turned = turn(q0_pieces)
-        take_out(0, 0, q0_turned)
-        store(0, 0, HALF)
-        v0_turned = turn(v0_pieces)
-        take_out(2, 0, v0_turned)
-        store(2, 0, HALF)
+        q_even = rotate(0, 0)
+        q_odd = rotate(0, 1)
+        k_even = rotate(1, 0)
+        k_odd = rotate(1, 1)
+        v_even = take_plain(0)
+        v_even_added = add_plain(v_even[0][0])
+        v_odd = take_plain(1)
+        v_odd_added = add_plain(v_odd[0][0])
         v_added = work.tile([P, P], F32, tag="v_added")
-        nc.gpsimd.tensor_tensor(out=v_added[:], in0=v0_added[:], in1=v1_added[:], op=ADD)
-        k0_turned = turn(k0_pieces)
-        take_out(1, 0, k0_turned)
-        store(1, 0, HALF)
-        q0_eighth = eighth(sum_rows(q0_turned))
-        k0_eighth = eighth(sum_rows(k0_turned))
-        q1_turned = turn(q1_pieces)
-        take_out(0, 1, q1_turned)
-        store(0, HALF, HALF)
-        mean(0, q0_eighth, sum_rows(q1_turned))
-        v1_turned = turn(v1_pieces)
+        nc.gpsimd.tensor_tensor(out=v_added[:], in0=v_even_added[:], in1=v_odd_added[:], op=ADD)
+        v_even_turned = turn(v_even)
+        take_out(2, 0, v_even_turned)
+        v_odd_turned = turn(v_odd)
+        take_out(2, 1, v_odd_turned)
+        store(2, 0, GROUP)
+        q_even_turned = turn(q_even)
+        take_out(0, 0, q_even_turned)
+        q_odd_turned = turn(q_odd)
+        take_out(0, 1, q_odd_turned)
+        store(0, 0, GROUP)
+        k_even_turned = turn(k_even)
+        take_out(1, 0, k_even_turned)
+        q_even_part = sum_rows(q_even_turned)
+        q_odd_part = sum_rows(q_odd_turned)
+        q_eighth = eighth(q_even_part)
+        k_even_part = sum_rows(k_even_turned)
+        mean(0, q_eighth, q_odd_part)
+        k_eighth = eighth(k_even_part)
+        k_odd_turned = turn(k_odd)
+        take_out(1, 1, k_odd_turned)
         v_sum = banks.tile([P, P], F32, tag="bank")
         nc.tensor.transpose(v_sum[:], v_added[:], identity[:])
-        take_out(2, 1, v1_turned)
         nc.scalar.mul(
             out=results[2][:, :, GROUP, :],
             in_=v_sum[:].rearrange("p (f c) -> p f c", c=HEAD),
             mul=1.0 / GROUP,
         )
-        store(2, HALF, HALF + 1)
+        store(1, 0, GROUP)
+        store(2, GROUP, 1)
         store(0, GROUP, 1)
-        k1_turned = turn(k1_pieces)
-        take_out(1, 1, k1_turned)
-        store(1, HALF, HALF)
-        k1_added = turn_and_add(k1_pieces)
-        mean(1, k0_eighth, k1_added)
+        k_odd_added = turn_and_add(k_odd)
+        mean(1, k_eighth, k_odd_added)
         store(1, GROUP, 1)

@@ -319,6 +319,10 @@ def tile_causalselfattention2_pa_s_kernel(
         k_eighth = eighth(k_even_part)
         k_odd_turned = turn(k_odd)
         take_out(1, 1, k_odd_turned)
+        store(1, 0, GROUP)
+        store(0, GROUP, 1)
+        k_odd_added = turn_and_add(k_odd)
+        mean(1, k_eighth, k_odd_added)
         v_sum = banks.tile([P, P], F32, tag="bank")
         nc.tensor.transpose(v_sum[:], v_added[:], identity[:])
         nc.scalar.mul(
@@ -326,9 +330,5 @@ def tile_causalselfattention2_pa_s_kernel(
             in_=v_sum[:].rearrange("p (f c) -> p f c", c=HEAD),
             mul=1.0 / GROUP,
         )
-        store(1, 0, GROUP)
-        store(2, GROUP, 1)
-        store(0, GROUP, 1)
-        k_odd_added = turn_and_add(k_odd)
-        mean(1, k_eighth, k_odd_added)
         store(1, GROUP, 1)
+        store(2, GROUP, 1)

@@ -49,14 +49,12 @@ def tile_causalselfattention2_pa_s_kernel(
         cos_rows = keep.tile([P, PAIRS], BF16)
         sin_rows = keep.tile([P, PAIRS], BF16)
         nc.scalar.dma_start(out=cos_rows[:], in_=freqs_cos)
-        nc.sync.dma_start(out=sin_rows[:], in_=freqs_sin)
+        nc.scalar.dma_start(out=sin_rows[:], in_=freqs_sin)
         x_rows = keep.tile([P, 2, CHANNELS], BF16)
         nc.sync.dma_start(
             out=x_rows[:].rearrange("p e k -> p (e k)"),
             in_=x.rearrange("b (q e) k -> (b q) (e k)", e=2),
         )
-        w_words = keep.tile([P, 2 * TENSORS * CHANNELS], U8, align_bytes=64)
-        nc.sync.dma_start(out=w_words[:].bitcast(I32), in_=w_attn_words[0].bitcast(I32))
 
         table_in = keep.tile([P, 1], F32)
         table_out = keep.tile([P, 1], F32)
@@ -70,6 +68,8 @@ def tile_causalselfattention2_pa_s_kernel(
                 out=w_scales[32 * quadrant : 32 * quadrant + 4, :].bitcast(I32),
                 in_=w_attn_scales[0, 4 * quadrant : 4 * quadrant + 4, :].bitcast(I32),
             )
+        w_words = keep.tile([P, 2 * TENSORS * CHANNELS], U8, align_bytes=64)
+        nc.sync.dma_start(out=w_words[:].bitcast(I32), in_=w_attn_words[0].bitcast(I32))
 
         identity = keep.tile([P, P], F32)
         make_identity(nc, identity[:])
@@ -138,6 +138,12 @@ def tile_causalselfattention2_pa_s_kernel(
                 .to_broadcast([P, GROUP, GROUPS, BATCH]),
             )
 
+        x_even_bank = turn_x(0)
+        x_odd_bank = turn_x(1)
+        nc.vector.tensor_copy(
+            out=x_grouped_words[:, parity_tokens(0)],
+            in_=x_even_bank[:].rearrange("p u n -> p n u"),
+        )
         nc.vector.tensor_copy(
             out=cos_wide[:],
             in_=cos_rows[:].unsqueeze(1).unsqueeze(3).to_broadcast([P, BLOCK_HEADS, PAIRS, 2]),
@@ -145,14 +151,8 @@ def tile_causalselfattention2_pa_s_kernel(
         sin_heads = sin_rows[:].unsqueeze(1).to_broadcast([P, BLOCK_HEADS, PAIRS])
         nc.vector.tensor_copy(out=sin_wide[:, :, :, 0], in_=sin_heads)
         nc.vector.tensor_scalar_mul(out=sin_wide[:, :, :, 1], in0=sin_heads, scalar1=-1.0)
-        x_even_bank = turn_x(0)
-        x_odd_bank = turn_x(1)
         turn_factor(0, cos_wide)
         turn_factor(1, sin_wide)
-        nc.vector.tensor_copy(
-            out=x_grouped_words[:, parity_tokens(0)],
-            in_=x_even_bank[:].rearrange("p u n -> p n u"),
-        )
         nc.scalar.copy(
             out=x_grouped_words[:, parity_tokens(1)],
             in_=x_odd_bank[:].rearrange("p u n -> p n u"),

from contextlib import ExitStack

import concourse.mybir as mybir
from concourse.masks import make_identity

F32 = mybir.dt.float32
BF16 = mybir.dt.bfloat16
I32 = mybir.dt.int32
U8 = mybir.dt.uint8
U32 = mybir.dt.uint32
FP8X4 = mybir.dt.float8_e4m3fn_x4
FP4X4 = mybir.dt.float4_e2m1fn_x4
MULT = mybir.AluOpType.mult
ADD = mybir.AluOpType.add
AXIS_X = mybir.AxisListType.X

P = 128
BATCH = 2
POSITIONS = 128
CHANNELS = 512
GROUPS = 16
GROUP = 8
HEAD = 32
PAIRS = HEAD // 2
BLOCK_HEADS = P // HEAD
HEAD_BLOCKS = CHANNELS // P
TENSORS = 3
ROTATED = 2
HALVES = 2
HALF = GROUP // HALVES
TOKENS = BATCH * POSITIONS
HALF_TOKENS = TOKENS // HALVES
assert HALF_TOKENS == P

FLOPS = 2 * TOKENS * CHANNELS * TENSORS * CHANNELS


def tile_causalselfattention2_pa_s_kernel(
    tc, x, w_attn_words, w_attn_scales, freqs_cos, freqs_sin, out_0, out_1, out_2
):
    nc = tc.nc
    outs = (out_0, out_1, out_2)
    with ExitStack() as ctx:
        keep = ctx.enter_context(tc.tile_pool(name="keep", bufs=1))
        work = ctx.enter_context(tc.tile_pool(name="work", bufs=ROTATED * HALVES))
        banks = ctx.enter_context(tc.psum_pool(name="banks", bufs=8))
        ctx.enter_context(tc.manual_schedule())

        cos_rows = keep.tile([P, PAIRS], BF16)
        sin_rows = keep.tile([P, PAIRS], BF16)
        nc.scalar.dma_start(out=cos_rows[:], in_=freqs_cos)
        nc.scalar.dma_start(out=sin_rows[:], in_=freqs_sin)
        x_rows = keep.tile([P, 2, CHANNELS], BF16)
        nc.sync.dma_start(
            out=x_rows[:].rearrange("p e k -> p (e k)"),
            in_=x.rearrange("b (q e) k -> (b q) (e k)", e=2),
        )

        table_in = keep.tile([P, 1], F32)
        table_out = keep.tile([P, 1], F32)
        nc.gpsimd.memset(table_in[:], 0.0)
        nc.scalar.copy(out=table_out[:], in_=table_in[:])

        w_scales = keep.tile([P, TENSORS * CHANNELS], U8, align_bytes=64)
        nc.vector.memset(w_scales[:].bitcast(I32), 0)
        for quadrant in range(4):
            nc.sync.dma_start(
                out=w_scales[32 * quadrant : 32 * quadrant + 4, :].bitcast(I32),
                in_=w_attn_scales[0, 4 * quadrant : 4 * quadrant + 4, :].bitcast(I32),
            )
        w_words = keep.tile([P, 2 * TENSORS * CHANNELS], U8, align_bytes=64)
        nc.sync.dma_start(out=w_words[:].bitcast(I32), in_=w_attn_words[0].bitcast(I32))

        identity = keep.tile([P, P], F32)
        make_identity(nc, identity[:])
        swap_pairs = keep.tile([P, P], F32)
        identity_pairs = identity[:].rearrange("p (m e) -> p m e", e=2)
        swapped_pairs = swap_pairs[:].rearrange("p (m e) -> p m e", e=2)
        sort_tokens = keep.tile([P, P], F32)
        nc.vector.tensor_copy(
            out=sort_tokens[:].rearrange("p (d g b) -> p d g b", d=HALF, g=GROUPS),
            in_=identity[:].rearrange("p (b g d) -> p d g b", b=BATCH, g=GROUPS),
        )
        nc.vector.tensor_copy(out=swapped_pairs[:, :, 0], in_=identity_pairs[:, :, 1])
        nc.vector.tensor_copy(out=swapped_pairs[:, :, 1], in_=identity_pairs[:, :, 0])

        x_grouped = keep.tile([P, TOKENS, 4], BF16, align_bytes=64)
        x_grouped_words = (
            x_grouped[:]
            .rearrange("p n t -> p (n t)")
            .bitcast(F32)
            .rearrange("p (n u) -> p n u", u=2)
        )
        x_codes = keep.tile([P, TOKENS], U32, align_bytes=64)
        x_scales = keep.tile([P, TOKENS], U8, align_bytes=64)

        def parity_tokens(e):
            return slice(HALF_TOKENS * e, HALF_TOKENS * (e + 1))

        def turn_x(e):
            x_bank = banks.tile([P, 2, HALF_TOKENS], F32, tag="bank")
            words = x_rows[:, e, :].bitcast(F32)
            for u in range(2):
                nc.tensor.matmul(
                    out=x_bank[:, u, :],
                    lhsT=words[:, u : CHANNELS // 2 : 2],
                    rhs=sort_tokens[:],
                    start=True,
                    stop=True,
                    is_transpose=True,
                )
            return x_bank

        def quantize_x(e):
            tokens = parity_tokens(e)
            nc.vector.quantize_mx(
                out=x_codes[:, tokens].bitcast(FP8X4),
                scales=x_scales[:, tokens],
                in_=x_grouped[:, tokens, :].rearrange("p n t -> p (n t)"),
            )

        cos_wide = keep.tile([P, BLOCK_HEADS, PAIRS, 2], F32)
        sin_wide = keep.tile([P, BLOCK_HEADS, PAIRS, 2], F32)
        factors_bank = banks.tile([P, 2, POSITIONS], F32, tag="bank")
        factors = keep.tile([P, 2, GROUP, GROUPS, BATCH], F32)

        def turn_factor(which, wide):
            nc.tensor.transpose(
                factors_bank[:, which, :], wide[:].rearrange("p f i e -> p (f i e)"), identity[:]
            )

        def spread_factor(which):
            nc.scalar.copy(
                out=factors[:, which],
                in_=factors_bank[:, which, :]
                .rearrange("p (g r) -> p r g", r=GROUP)
                .unsqueeze(3)
                .to_broadcast([P, GROUP, GROUPS, BATCH]),
            )

        x_even_bank = turn_x(0)
        x_odd_bank = turn_x(1)
        nc.vector.tensor_copy(
            out=x_grouped_words[:, parity_tokens(0)],
            in_=x_even_bank[:].rearrange("p u n -> p n u"),
        )
        nc.vector.tensor_copy(
            out=cos_wide[:],
            in_=cos_rows[:].unsqueeze(1).unsqueeze(3).to_broadcast([P, BLOCK_HEADS, PAIRS, 2]),
        )
        sin_heads = sin_rows[:].unsqueeze(1).to_broadcast([P, BLOCK_HEADS, PAIRS])
        nc.vector.tensor_copy(out=sin_wide[:, :, :, 0], in_=sin_heads)
        nc.vector.tensor_scalar_mul(out=sin_wide[:, :, :, 1], in0=sin_heads, scalar1=-1.0)
        turn_factor(0, cos_wide)
        turn_factor(1, sin_wide)
        nc.scalar.copy(
            out=x_grouped_words[:, parity_tokens(1)],
            in_=x_odd_bank[:].rearrange("p u n -> p n u"),
        )
        quantize_x(0)
        quantize_x(1)
        spread_factor(0)
        spread_factor(1)

        products = {}

        def multiply(s, e):
            tokens = parity_tokens(e)
            product = banks.tile([P, HEAD_BLOCKS, HALF_TOKENS], F32, tag="bank")
            for j in range(HEAD_BLOCKS):
                first = CHANNELS * s + P * j
                nc.tensor.matmul_mx(
                    out=product[:, j, :],
                    lhsT=w_words[:, 2 * first : 2 * (first + P)].bitcast(FP4X4),
                    lhsT_scale=w_scales[:, first : first + P],
                    rhs=x_codes[:, tokens].bitcast(FP8X4),
                    rhs_scale=x_scales[:, tokens],
                    start=True,
                    stop=True,
                )
            products[(s, e)] = product

        def sorted_product(s, e):
            return products[(s, e)][:].rearrange("p j (d n) -> p d n j", d=HALF)

        def take_plain(e):
            plain = work.tile([P, HALF, P], F32, tag="plain")
            nc.scalar.copy(
                out=plain[:].rearrange("p d (n j) -> p d n j", j=HEAD_BLOCKS),
                in_=sorted_product(2, e),
            )
            return [(plain, identity)]

        def rotate(s, e):
            pieces = []
            for which, permutation in ((0, identity), (1, swap_pairs)):
                factor = (
                    factors[:, which, e:GROUP:2]
                    .rearrange("p d g b -> p d (g b)")
                    .unsqueeze(3)
                    .to_broadcast([P, HALF, GROUPS * BATCH, HEAD_BLOCKS])
                )
                scaled = work.tile([P, HALF, P], F32, tag="scaled%d" % which)
                nc.vector.tensor_tensor(
                    out=scaled[:].rearrange("p d (n j) -> p d n j", j=HEAD_BLOCKS),
                    in0=sorted_product(s, e),
                    in1=factor,
                    op=MULT,
                )
                pieces.append((scaled, permutation))
            return pieces

        results = []
        for s in range(TENSORS):
            result = keep.tile([P, BLOCK_HEADS, GROUP + 1, HEAD], F32, name="result%d" % s)
            results.append(result)

        def store(s, first_row, rows):
            nc.sync.dma_start(
                out=outs[s][:, :, :, first_row : first_row + rows, :].rearrange(
                    "b h g r c -> g (b h) (r c)"
                ),
                in_=results[s][:, :, first_row : first_row + rows, :].rearrange(
                    "p f r c -> p f (r c)"
                ),
            )

        def transpose_into(out, piece, permutation, start, stop):
            nc.tensor.matmul(
                out=out, lhsT=piece, rhs=permutation[:], start=start, stop=stop, is_transpose=True
            )

        def turn(pieces):
            turned = banks.tile([P, HALF, P], F32, tag="bank")
            for d in range(HALF):
                for n, (piece, permutation) in enumerate(pieces):
                    transpose_into(
                        turned[:, d, :], piece[:, d, :], permutation, n == 0, n == len(pieces) - 1
                    )
            return turned

        def turn_and_add(pieces):
            added = banks.tile([P, P], F32, tag="bank")
            steps = [(piece, d, permutation) for d in range(HALF) for piece, permutation in pieces]
            for n, (piece, d, permutation) in enumerate(steps):
                transpose_into(added[:], piece[:, d, :], permutation, n == 0, n == len(steps) - 1)
            return added

        def take_out(s, e, turned):
            nc.scalar.copy(
                out=results[s][:, :, e:GROUP:2, :].rearrange("p f r c -> p r f c"),
                in_=turned[:].rearrange("p r (f c) -> p r f c", c=HEAD),
            )

        def add_plain(plain):
            pairs = work.tile([P, 2, P], F32, tag="pairs")
            nc.gpsimd.tensor_tensor(
                out=pairs[:], in0=plain[:, 0:2, :], in1=plain[:, 2:4, :], op=ADD
            )
            four = work.tile([P, P], F32, tag="four")
            nc.gpsimd.tensor_tensor(out=four[:], in0=pairs[:, 0, :], in1=pairs[:, 1, :], op=ADD)
            return four

        def sum_rows(turned):
            part = work.tile([P, P], F32, tag="part")
            nc.vector.tensor_reduce(
                out=part[:], in_=turned[:].rearrange("p r m -> p m r"), axis=AXIS_X, op=ADD
            )
            return part

        def eighth(part):
            scaled_part = work.tile([P, P], F32, tag="scaled_part")
            nc.vector.tensor_scalar_mul(out=scaled_part[:], in0=part[:], scalar1=1.0 / GROUP)
            return scaled_part

        def mean(s, first_eighth, second_part):
            nc.vector.scalar_tensor_tensor(
                out=results[s][:, :, GROUP, :],
                in0=second_part[:].rearrange("p (f c) -> p f c", c=HEAD),
                scalar=1.0 / GROUP,
                in1=first_eighth[:].rearrange("p (f c) -> p f c", c=HEAD),
                op0=MULT,
                op1=ADD,
            )

        multiply(0, 0)
        multiply(0, 1)
        multiply(2, 0)
        multiply(2, 1)
        multiply(1, 0)
        multiply(1, 1)
        q_even = rotate(0, 0)
        q_odd = rotate(0, 1)
        k_even = rotate(1, 0)
        k_odd = rotate(1, 1)
        v_even = take_plain(0)
        v_even_added = add_plain(v_even[0][0])
        v_odd = take_plain(1)
        v_odd_added = add_plain(v_odd[0][0])
        v_added = work.tile([P, P], F32, tag="v_added")
        nc.gpsimd.tensor_tensor(out=v_added[:], in0=v_even_added[:], in1=v_odd_added[:], op=ADD)
        v_even_turned = turn(v_even)
        take_out(2, 0, v_even_turned)
        v_odd_turned = turn(v_odd)
        take_out(2, 1, v_odd_turned)
        store(2, 0, GROUP)
        q_even_turned = turn(q_even)
        take_out(0, 0, q_even_turned)
        q_odd_turned = turn(q_odd)
        take_out(0, 1, q_odd_turned)
        store(0, 0, GROUP)
        k_even_turned = turn(k_even)
        take_out(1, 0, k_even_turned)
        q_even_part = sum_rows(q_even_turned)
        q_odd_part = sum_rows(q_odd_turned)
        q_eighth = eighth(q_even_part)
        k_even_part = sum_rows(k_even_turned)
        mean(0, q_eighth, q_odd_part)
        k_eighth = eighth(k_even_part)
        k_odd_turned = turn(k_odd)
        take_out(1, 1, k_odd_turned)
        store(1, 0, GROUP)
        store(0, GROUP, 1)
        k_odd_added = turn_and_add(k_odd)
        mean(1, k_eighth, k_odd_added)
        v_sum = banks.tile([P, P], F32, tag="bank")
        nc.tensor.transpose(v_sum[:], v_added[:], identity[:])
        nc.scalar.mul(
            out=results[2][:, :, GROUP, :],
            in_=v_sum[:].rearrange("p (f c) -> p f c", c=HEAD),
            mul=1.0 / GROUP,
        )
        store(1, GROUP, 1)
        store(2, GROUP, 1)
